import numpy as np
import ml_dtypes

BF16 = ml_dtypes.bfloat16


def bf(x):
    return np.asarray(x, np.float32).astype(BF16)


def f32(x):
    return np.asarray(x, np.float32)


def f64(x):
    return np.asarray(x).astype(np.float64)


def striped(idx):
    return np.tile(idx.reshape(-1, 16).T, (8, 1))


C, S, N, H, M = 128, 4096, 4096, 512, 128
CLAMP = 2.0


def silu(v):
    return v / (1.0 + np.exp(-v))


def setup_inputs():
    amp = np.random.uniform(0.1, 0.5, (1, S))
    return {
        "t_store": f32(np.random.standard_normal((C, S)) * amp),
        "w_in": bf(np.random.standard_normal((C, H))),
        "b_in": f32(0.1 * np.random.standard_normal((H, 1))),
        "w_out": bf(np.random.standard_normal((H, M)) / np.sqrt(H)),
        "b_out": f32(0.1 * np.random.standard_normal((M, 1))),
        "offs": striped(np.random.permutation(np.tile(np.arange(S), 2))[:N]),
    }


def reference(t_store, w_in, b_in, w_out, b_out, offs):
    idx = offs[:16].T.reshape(-1)
    t = f64(t_store)[:, idx]
    norm = np.sqrt(np.sum(t * t, axis=0, keepdims=True))
    h = silu(f64(w_in).T @ (t / norm) + f64(b_in))
    y = (f64(w_out).T @ h + f64(b_out)) * np.sqrt(norm)
    return np.minimum(np.maximum(y, -CLAMP), CLAMP)

@@ -1,0 +1,118 @@
+import concourse.mybir as mybir
+from concourse.masks import make_identity
+
+F32 = mybir.dt.float32
+BF16 = mybir.dt.bfloat16
+U16 = mybir.dt.uint16
+ACT = mybir.ActivationFunctionType
+ALU = mybir.AluOpType
+
+P = 128
+C, S, N, H, M = 128, 4096, 4096, 512, 128
+CLAMP = 2.0
+PIECE = 512
+N_PIECES = N // PIECE
+BLOCKS = PIECE // P
+H_BLOCKS = H // P
+FLOPS = 2 * N * (C * H + H * M)
+
+
+def tile_qdtssolveronnx_kernel(tc, t_store, w_in, b_in, w_out, b_out, offs, out):
+    nc = tc.nc
+    with (
+        tc.tile_pool(name="held", bufs=1) as held,
+        tc.tile_pool(name="per_piece", bufs=N_PIECES) as per_piece,
+        tc.tile_pool(name="ring", bufs=3) as ring,
+        tc.psum_pool(name="psum", bufs=1) as psum,
+    ):
+        offsets = held.tile([P, N // 16], U16, name="offsets")
+        nc.sync.dma_start(offsets[:], offs)
+        store = held.tile([C, S], F32, name="store")
+        nc.sync.dma_start(store[:], t_store)
+
+        w_in_sb = held.tile([C, H], BF16, name="w_in_sb")
+        nc.scalar.dma_start(w_in_sb[:], w_in)
+        w_out_sb = held.tile([P, H_BLOCKS, M], BF16, name="w_out_sb")
+        nc.scalar.dma_start(w_out_sb[:], w_out.rearrange("(k p) m -> p k m", p=P))
+        b_in_sb = held.tile([P, H_BLOCKS], F32, name="b_in_sb")
+        b_out_sb = held.tile([M, 1], F32, name="b_out_sb")
+        with nc.allow_non_contiguous_dma(reason="a bias has one element to a partition"):
+            nc.scalar.dma_start(b_in_sb[:], b_in.rearrange("(k p) o -> p (k o)", p=P))
+            nc.scalar.dma_start(b_out_sb[:], b_out)
+
+        ones_col = held.tile([C, 1], BF16, name="ones_col")
+        nc.vector.memset(ones_col[:], 1.0)
+        exponents = held.tile([P, 2, BLOCKS], F32, name="exponents")
+        nc.vector.memset(exponents[:, 0, :], -0.5)
+        nc.vector.memset(exponents[:, 1, :], 0.25)
+        identity = held.tile([P, P], F32, name="identity")
+        make_identity(nc, identity[:])
+
+        unit = []
+        root = []
+        for i in range(N_PIECES):
+            picked = per_piece.tile([C, PIECE], F32, name="picked")
+            nc.scalar.activation(
+                picked[:],
+                store[:].indirect(offsets[:, i * (PIECE // 16) : (i + 1) * (PIECE // 16)]),
+                ACT.Copy,
+            )
+
+            squares = ring.tile([C, PIECE], BF16, name="squares")
+            nc.vector.tensor_tensor(squares[:], picked[:], picked[:], ALU.mult)
+
+            sums_ps = psum.tile([P, BLOCKS], F32, name="sums_ps")
+            for b in range(BLOCKS):
+                nc.tensor.matmul(
+                    sums_ps[:, b : b + 1],
+                    lhsT=squares[:, b * P : (b + 1) * P],
+                    rhs=ones_col[:],
+                    start=True,
+                    stop=True,
+                )
+            sums = ring.tile([P, 2, BLOCKS], F32, name="sums")
+            nc.vector.tensor_copy(sums[:], sums_ps[:].unsqueeze(1).to_broadcast([P, 2, BLOCKS]))
+            powers = ring.tile([P, 2, BLOCKS], F32, name="powers")
+            nc.gpsimd.tensor_tensor(powers[:], sums[:], exponents[:], ALU.pow)
+
+            spread = []
+            for q in range(2):
+                spread_ps = psum.tile([P, PIECE], F32, name="spread_ps", bufs=2)
+                for b in range(BLOCKS):
+                    nc.tensor.transpose(
+                        spread_ps[:, b * P : (b + 1) * P],
+                        powers[:, q, b : b + 1].to_broadcast([P, P]),
+                        identity[:],
+                    )
+                spread.append(spread_ps)
+
+            unit_i = per_piece.tile([C, PIECE], BF16, name="unit_i")
+            nc.vector.tensor_tensor(unit_i[:], picked[:], spread[0][:], ALU.mult)
+            unit.append(unit_i)
+            root_i = per_piece.tile([M, PIECE], F32, name="root_i")
+            nc.vector.tensor_copy(root_i[:], spread[1][:])
+            root.append(root_i)
+
+        for i in range(N_PIECES):
+            y_ps = psum.tile([M, PIECE], F32, name="y_ps")
+            for k in range(H_BLOCKS):
+                z_ps = psum.tile([P, PIECE], F32, name="z_ps", bufs=4)
+                nc.tensor.matmul(
+                    z_ps[:], lhsT=w_in_sb[:, k * P : (k + 1) * P], rhs=unit[i][:], start=True, stop=True
+                )
+                hidden = per_piece.tile([P, PIECE], BF16, name="hidden")
+                nc.scalar.activation(hidden[:], z_ps[:], ACT.Silu, bias=b_in_sb[:, k : k + 1])
+                nc.tensor.matmul(
+                    y_ps[:],
+                    lhsT=w_out_sb[:, k, :],
+                    rhs=hidden[:],
+                    start=(k == 0),
+                    stop=(k == H_BLOCKS - 1),
+                )
+            scaled = ring.tile([M, PIECE], F32, name="scaled")
+            nc.vector.scalar_tensor_tensor(
+                scaled[:], in0=y_ps[:], scalar=b_out_sb[:, 0:1], in1=root[i][:], op0=ALU.add, op1=ALU.mult
+            )
+            clamped = ring.tile([M, PIECE], F32, name="clamped")
+            nc.vector.tensor_scalar(clamped[:], scaled[:], -CLAMP, CLAMP, op0=ALU.max, op1=ALU.min)
+            nc.sync.dma_start(out[:, i * PIECE : (i + 1) * PIECE], clamped[:])

@@ -16,6 +16,9 @@ BLOCKS = PIECE // P
 H_BLOCKS = H // P
 FLOPS = 2 * N * (C * H + H * M)
 
+NORMALISE_LAG = 2
+NETWORK_LAG = 5
+
 
 def tile_qdtssolveronnx_kernel(tc, t_store, w_in, b_in, w_out, b_out, offs, out):
     nc = tc.nc
@@ -28,16 +31,17 @@ def tile_qdtssolveronnx_kernel(tc, t_store, w_in, b_in, w_out, b_out, offs, out)
         offsets = held.tile([P, N // 16], U16, name="offsets")
         nc.sync.dma_start(offsets[:], offs)
         store = held.tile([C, S], F32, name="store")
-        nc.sync.dma_start(store[:], t_store)
+        nc.sync.dma_start(store[:, : S // 2], t_store[:, : S // 2])
+        nc.scalar.dma_start(store[:, S // 2 :], t_store[:, S // 2 :])
 
         w_in_sb = held.tile([C, H], BF16, name="w_in_sb")
-        nc.scalar.dma_start(w_in_sb[:], w_in)
+        nc.sync.dma_start(w_in_sb[:], w_in)
         w_out_sb = held.tile([P, H_BLOCKS, M], BF16, name="w_out_sb")
         nc.scalar.dma_start(w_out_sb[:], w_out.rearrange("(k p) m -> p k m", p=P))
         b_in_sb = held.tile([P, H_BLOCKS], F32, name="b_in_sb")
         b_out_sb = held.tile([M, 1], F32, name="b_out_sb")
         with nc.allow_non_contiguous_dma(reason="a bias has one element to a partition"):
-            nc.scalar.dma_start(b_in_sb[:], b_in.rearrange("(k p) o -> p (k o)", p=P))
+            nc.sync.dma_start(b_in_sb[:], b_in.rearrange("(k p) o -> p (k o)", p=P))
             nc.scalar.dma_start(b_out_sb[:], b_out)
 
         ones_col = held.tile([C, 1], BF16, name="ones_col")
@@ -48,19 +52,21 @@ def tile_qdtssolveronnx_kernel(tc, t_store, w_in, b_in, w_out, b_out, offs, out)
         identity = held.tile([P, P], F32, name="identity")
         make_identity(nc, identity[:])
 
-        unit = []
-        root = []
-        for i in range(N_PIECES):
-            picked = per_piece.tile([C, PIECE], F32, name="picked")
+        picked = {}
+        powers = {}
+        unit = {}
+        root = {}
+        z_ps = {}
+
+        def pick(i):
+            picked[i] = per_piece.tile([C, PIECE], F32, name="picked")
             nc.scalar.activation(
-                picked[:],
+                picked[i][:],
                 store[:].indirect(offsets[:, i * (PIECE // 16) : (i + 1) * (PIECE // 16)]),
                 ACT.Copy,
             )
-
             squares = ring.tile([C, PIECE], BF16, name="squares")
-            nc.vector.tensor_tensor(squares[:], picked[:], picked[:], ALU.mult)
-
+            nc.vector.tensor_tensor(squares[:], picked[i][:], picked[i][:], ALU.mult)
             sums_ps = psum.tile([P, BLOCKS], F32, name="sums_ps")
             for b in range(BLOCKS):
                 nc.tensor.matmul(
@@ -72,36 +78,36 @@ def tile_qdtssolveronnx_kernel(tc, t_store, w_in, b_in, w_out, b_out, offs, out)
                 )
             sums = ring.tile([P, 2, BLOCKS], F32, name="sums")
             nc.vector.tensor_copy(sums[:], sums_ps[:].unsqueeze(1).to_broadcast([P, 2, BLOCKS]))
-            powers = ring.tile([P, 2, BLOCKS], F32, name="powers")
-            nc.gpsimd.tensor_tensor(powers[:], sums[:], exponents[:], ALU.pow)
+            powers[i] = ring.tile([P, 2, BLOCKS], F32, name="powers", bufs=NORMALISE_LAG + 2)
+            nc.gpsimd.tensor_tensor(powers[i][:], sums[:], exponents[:], ALU.pow)
 
+        def normalise(i):
             spread = []
             for q in range(2):
                 spread_ps = psum.tile([P, PIECE], F32, name="spread_ps", bufs=2)
                 for b in range(BLOCKS):
                     nc.tensor.transpose(
                         spread_ps[:, b * P : (b + 1) * P],
-                        powers[:, q, b : b + 1].to_broadcast([P, P]),
+                        powers[i][:, q, b : b + 1].to_broadcast([P, P]),
                         identity[:],
                     )
                 spread.append(spread_ps)
+            unit[i] = per_piece.tile([C, PIECE], BF16, name="unit")
+            nc.vector.tensor_tensor(unit[i][:], picked[i][:], spread[0][:], ALU.mult)
+            root[i] = per_piece.tile([M, PIECE], F32, name="root")
+            nc.vector.tensor_copy(root[i][:], spread[1][:])
 
-            unit_i = per_piece.tile([C, PIECE], BF16, name="unit_i")
-            nc.vector.tensor_tensor(unit_i[:], picked[:], spread[0][:], ALU.mult)
-            unit.append(unit_i)
-            root_i = per_piece.tile([M, PIECE], F32, name="root_i")
-            nc.vector.tensor_copy(root_i[:], spread[1][:])
-            root.append(root_i)
+        def first_product(i, k):
+            z_ps[i, k] = psum.tile([P, PIECE], F32, name="z_ps", bufs=H_BLOCKS)
+            nc.tensor.matmul(
+                z_ps[i, k][:], lhsT=w_in_sb[:, k * P : (k + 1) * P], rhs=unit[i][:], start=True, stop=True
+            )
 
-        for i in range(N_PIECES):
+        def network(i):
             y_ps = psum.tile([M, PIECE], F32, name="y_ps")
             for k in range(H_BLOCKS):
-                z_ps = psum.tile([P, PIECE], F32, name="z_ps", bufs=4)
-                nc.tensor.matmul(
-                    z_ps[:], lhsT=w_in_sb[:, k * P : (k + 1) * P], rhs=unit[i][:], start=True, stop=True
-                )
                 hidden = per_piece.tile([P, PIECE], BF16, name="hidden")
-                nc.scalar.activation(hidden[:], z_ps[:], ACT.Silu, bias=b_in_sb[:, k : k + 1])
+                nc.scalar.activation(hidden[:], z_ps[i, k][:], ACT.Silu, bias=b_in_sb[:, k : k + 1])
                 nc.tensor.matmul(
                     y_ps[:],
                     lhsT=w_out_sb[:, k, :],
@@ -109,6 +115,8 @@ def tile_qdtssolveronnx_kernel(tc, t_store, w_in, b_in, w_out, b_out, offs, out)
                     start=(k == 0),
                     stop=(k == H_BLOCKS - 1),
                 )
+                if i + 1 < N_PIECES:
+                    first_product(i + 1, k)
             scaled = ring.tile([M, PIECE], F32, name="scaled")
             nc.vector.scalar_tensor_tensor(
                 scaled[:], in0=y_ps[:], scalar=b_out_sb[:, 0:1], in1=root[i][:], op0=ALU.add, op1=ALU.mult
@@ -116,3 +124,14 @@ def tile_qdtssolveronnx_kernel(tc, t_store, w_in, b_in, w_out, b_out, offs, out)
             clamped = ring.tile([M, PIECE], F32, name="clamped")
             nc.vector.tensor_scalar(clamped[:], scaled[:], -CLAMP, CLAMP, op0=ALU.max, op1=ALU.min)
             nc.sync.dma_start(out[:, i * PIECE : (i + 1) * PIECE], clamped[:])
+
+        for step in range(N_PIECES + NETWORK_LAG):
+            if step < N_PIECES:
+                pick(step)
+            if 0 <= step - NORMALISE_LAG < N_PIECES:
+                normalise(step - NORMALISE_LAG)
+            if step == NORMALISE_LAG:
+                for k in range(H_BLOCKS):
+                    first_product(0, k)
+            if step >= NETWORK_LAG:
+                network(step - NETWORK_LAG)

@@ -17,7 +17,7 @@ H_BLOCKS = H // P
 FLOPS = 2 * N * (C * H + H * M)
 
 NORMALISE_LAG = 2
-NETWORK_LAG = 5
+NETWORK_LAG = 4
 
 
 def tile_qdtssolveronnx_kernel(tc, t_store, w_in, b_in, w_out, b_out, offs, out):
@@ -46,11 +46,13 @@ def tile_qdtssolveronnx_kernel(tc, t_store, w_in, b_in, w_out, b_out, offs, out)
 
         ones_col = held.tile([C, 1], BF16, name="ones_col")
         nc.vector.memset(ones_col[:], 1.0)
-        exponents = held.tile([P, 2, BLOCKS], F32, name="exponents")
-        nc.vector.memset(exponents[:, 0, :], -0.5)
-        nc.vector.memset(exponents[:, 1, :], 0.25)
+        exponent = held.tile([P, BLOCKS], F32, name="exponent")
+        nc.vector.memset(exponent[:], -0.25)
         identity = held.tile([P, P], F32, name="identity")
         make_identity(nc, identity[:])
+
+        warm = held.tile([P, 1], F32, name="warm")
+        nc.scalar.activation(warm[:], exponent[:, 0:1], ACT.Silu)
 
         picked = {}
         powers = {}
@@ -76,10 +78,15 @@ def tile_qdtssolveronnx_kernel(tc, t_store, w_in, b_in, w_out, b_out, offs, out)
                     start=True,
                     stop=True,
                 )
-            sums = ring.tile([P, 2, BLOCKS], F32, name="sums")
-            nc.vector.tensor_copy(sums[:], sums_ps[:].unsqueeze(1).to_broadcast([P, 2, BLOCKS]))
-            powers[i] = ring.tile([P, 2, BLOCKS], F32, name="powers", bufs=NORMALISE_LAG + 2)
-            nc.gpsimd.tensor_tensor(powers[i][:], sums[:], exponents[:], ALU.pow)
+            sums = per_piece.tile([P, BLOCKS], F32, name="sums")
+            nc.vector.tensor_copy(sums[:], sums_ps[:])
+            quarter = per_piece.tile([P, BLOCKS], F32, name="quarter")
+            nc.gpsimd.tensor_tensor(quarter[:], sums[:], exponent[:], ALU.pow)
+            powers[i] = per_piece.tile([P, 2, BLOCKS], F32, name="powers")
+            three_quarters = per_piece.tile([P, BLOCKS], F32, name="three_quarters")
+            nc.vector.tensor_tensor(powers[i][:, 0, :], quarter[:], quarter[:], ALU.mult)
+            nc.vector.tensor_tensor(three_quarters[:], sums[:], quarter[:], ALU.mult)
+            nc.vector.tensor_tensor(powers[i][:, 1, :], three_quarters[:], powers[i][:, 0, :], ALU.mult)
 
         def normalise(i):
             spread = []
@@ -126,6 +133,8 @@ def tile_qdtssolveronnx_kernel(tc, t_store, w_in, b_in, w_out, b_out, offs, out)
             nc.sync.dma_start(out[:, i * PIECE : (i + 1) * PIECE], clamped[:])
 
         for step in range(N_PIECES + NETWORK_LAG):
+            if step >= NETWORK_LAG:
+                network(step - NETWORK_LAG)
             if step < N_PIECES:
                 pick(step)
             if 0 <= step - NORMALISE_LAG < N_PIECES:
@@ -133,5 +142,3 @@ def tile_qdtssolveronnx_kernel(tc, t_store, w_in, b_in, w_out, b_out, offs, out)
             if step == NORMALISE_LAG:
                 for k in range(H_BLOCKS):
                     first_product(0, k)
-            if step >= NETWORK_LAG:
-                network(step - NETWORK_LAG)

@@ -17,7 +17,7 @@ H_BLOCKS = H // P
 FLOPS = 2 * N * (C * H + H * M)
 
 NORMALISE_LAG = 2
-NETWORK_LAG = 4
+NETWORK_LAG = 5
 
 
 def tile_qdtssolveronnx_kernel(tc, t_store, w_in, b_in, w_out, b_out, offs, out):
@@ -46,13 +46,14 @@ def tile_qdtssolveronnx_kernel(tc, t_store, w_in, b_in, w_out, b_out, offs, out)
 
         ones_col = held.tile([C, 1], BF16, name="ones_col")
         nc.vector.memset(ones_col[:], 1.0)
-        exponent = held.tile([P, BLOCKS], F32, name="exponent")
-        nc.vector.memset(exponent[:], -0.25)
+        exponents = held.tile([P, 2, BLOCKS], F32, name="exponents")
+        nc.vector.memset(exponents[:, 0, :], -0.5)
+        nc.vector.memset(exponents[:, 1, :], 0.25)
         identity = held.tile([P, P], F32, name="identity")
         make_identity(nc, identity[:])
 
         warm = held.tile([P, 1], F32, name="warm")
-        nc.scalar.activation(warm[:], exponent[:, 0:1], ACT.Silu)
+        nc.scalar.activation(warm[:], exponents[:, 0, 0:1], ACT.Silu)
 
         picked = {}
         powers = {}
@@ -78,15 +79,10 @@ def tile_qdtssolveronnx_kernel(tc, t_store, w_in, b_in, w_out, b_out, offs, out)
                     start=True,
                     stop=True,
                 )
-            sums = per_piece.tile([P, BLOCKS], F32, name="sums")
-            nc.vector.tensor_copy(sums[:], sums_ps[:])
-            quarter = per_piece.tile([P, BLOCKS], F32, name="quarter")
-            nc.gpsimd.tensor_tensor(quarter[:], sums[:], exponent[:], ALU.pow)
-            powers[i] = per_piece.tile([P, 2, BLOCKS], F32, name="powers")
-            three_quarters = per_piece.tile([P, BLOCKS], F32, name="three_quarters")
-            nc.vector.tensor_tensor(powers[i][:, 0, :], quarter[:], quarter[:], ALU.mult)
-            nc.vector.tensor_tensor(three_quarters[:], sums[:], quarter[:], ALU.mult)
-            nc.vector.tensor_tensor(powers[i][:, 1, :], three_quarters[:], powers[i][:, 0, :], ALU.mult)
+            sums = ring.tile([P, 2, BLOCKS], F32, name="sums")
+            nc.vector.tensor_copy(sums[:], sums_ps[:].unsqueeze(1).to_broadcast([P, 2, BLOCKS]))
+            powers[i] = ring.tile([P, 2, BLOCKS], F32, name="powers", bufs=NORMALISE_LAG + 2)
+            nc.gpsimd.tensor_tensor(powers[i][:], sums[:], exponents[:], ALU.pow)
 
         def normalise(i):
             spread = []
@@ -133,8 +129,6 @@ def tile_qdtssolveronnx_kernel(tc, t_store, w_in, b_in, w_out, b_out, offs, out)
             nc.sync.dma_start(out[:, i * PIECE : (i + 1) * PIECE], clamped[:])
 
         for step in range(N_PIECES + NETWORK_LAG):
-            if step >= NETWORK_LAG:
-                network(step - NETWORK_LAG)
             if step < N_PIECES:
                 pick(step)
             if 0 <= step - NORMALISE_LAG < N_PIECES:
@@ -142,3 +136,5 @@ def tile_qdtssolveronnx_kernel(tc, t_store, w_in, b_in, w_out, b_out, offs, out)
             if step == NORMALISE_LAG:
                 for k in range(H_BLOCKS):
                     first_product(0, k)
+            if step >= NETWORK_LAG:
+                network(step - NETWORK_LAG)

@@ -15,6 +15,7 @@ N_PIECES = N // PIECE
 BLOCKS = PIECE // P
 H_BLOCKS = H // P
 FLOPS = 2 * N * (C * H + H * M)
+PARK = slice(N - 2 * BLOCKS * P, N)
 
 NORMALISE_LAG = 2
 NETWORK_LAG = 5
@@ -30,19 +31,18 @@ def tile_qdtssolveronnx_kernel(tc, t_store, w_in, b_in, w_out, b_out, offs, out)
     ):
         offsets = held.tile([P, N // 16], U16, name="offsets")
         nc.sync.dma_start(offsets[:], offs)
-        store = held.tile([C, S], F32, name="store")
-        nc.sync.dma_start(store[:, : S // 2], t_store[:, : S // 2])
-        nc.scalar.dma_start(store[:, S // 2 :], t_store[:, S // 2 :])
-
-        w_in_sb = held.tile([C, H], BF16, name="w_in_sb")
-        nc.sync.dma_start(w_in_sb[:], w_in)
-        w_out_sb = held.tile([P, H_BLOCKS, M], BF16, name="w_out_sb")
-        nc.scalar.dma_start(w_out_sb[:], w_out.rearrange("(k p) m -> p k m", p=P))
         b_in_sb = held.tile([P, H_BLOCKS], F32, name="b_in_sb")
         b_out_sb = held.tile([M, 1], F32, name="b_out_sb")
         with nc.allow_non_contiguous_dma(reason="a bias has one element to a partition"):
             nc.sync.dma_start(b_in_sb[:], b_in.rearrange("(k p) o -> p (k o)", p=P))
             nc.scalar.dma_start(b_out_sb[:], b_out)
+        w_in_sb = held.tile([C, H], BF16, name="w_in_sb")
+        nc.sync.dma_start(w_in_sb[:], w_in)
+        w_out_sb = held.tile([P, H_BLOCKS, M], BF16, name="w_out_sb")
+        nc.scalar.dma_start(w_out_sb[:], w_out.rearrange("(k p) m -> p k m", p=P))
+        store = held.tile([C, S], F32, name="store")
+        nc.sync.dma_start(store[:, : S // 2], t_store[:, : S // 2])
+        nc.scalar.dma_start(store[:, S // 2 :], t_store[:, S // 2 :])
 
         ones_col = held.tile([C, 1], BF16, name="ones_col")
         nc.vector.memset(ones_col[:], 1.0)
@@ -58,8 +58,11 @@ def tile_qdtssolveronnx_kernel(tc, t_store, w_in, b_in, w_out, b_out, offs, out)
         picked = {}
         powers = {}
         unit = {}
-        root = {}
+        both = {}
         z_ps = {}
+
+        def columns(i):
+            return slice(i * PIECE, (i + 1) * PIECE)
 
         def pick(i):
             picked[i] = per_piece.tile([C, PIECE], F32, name="picked")
@@ -81,24 +84,24 @@ def tile_qdtssolveronnx_kernel(tc, t_store, w_in, b_in, w_out, b_out, offs, out)
                 )
             sums = ring.tile([P, 2, BLOCKS], F32, name="sums")
             nc.vector.tensor_copy(sums[:], sums_ps[:].unsqueeze(1).to_broadcast([P, 2, BLOCKS]))
-            powers[i] = ring.tile([P, 2, BLOCKS], F32, name="powers", bufs=NORMALISE_LAG + 2)
+            powers[i] = per_piece.tile([P, 2, BLOCKS], F32, name="powers")
             nc.gpsimd.tensor_tensor(powers[i][:], sums[:], exponents[:], ALU.pow)
+            nc.sync.dma_start(
+                out[i : i + 1, PARK].rearrange("o (p e) -> (o p) e", e=2 * BLOCKS), powers[i][:]
+            )
 
         def normalise(i):
-            spread = []
-            for q in range(2):
-                spread_ps = psum.tile([P, PIECE], F32, name="spread_ps", bufs=2)
-                for b in range(BLOCKS):
-                    nc.tensor.transpose(
-                        spread_ps[:, b * P : (b + 1) * P],
-                        powers[i][:, q, b : b + 1].to_broadcast([P, P]),
-                        identity[:],
-                    )
-                spread.append(spread_ps)
+            both[i] = per_piece.tile([M, P, 2, BLOCKS], F32, name="both")
+            nc.sync.dma_start(both[i][:], out[i, PARK].partition_broadcast(M))
+            spread_ps = psum.tile([P, PIECE], F32, name="spread_ps", bufs=2)
+            for b in range(BLOCKS):
+                nc.tensor.transpose(
+                    spread_ps[:, b * P : (b + 1) * P],
+                    powers[i][:, 0, b : b + 1].to_broadcast([P, P]),
+                    identity[:],
+                )
             unit[i] = per_piece.tile([C, PIECE], BF16, name="unit")
-            nc.vector.tensor_tensor(unit[i][:], picked[i][:], spread[0][:], ALU.mult)
-            root[i] = per_piece.tile([M, PIECE], F32, name="root")
-            nc.vector.tensor_copy(root[i][:], spread[1][:])
+            nc.vector.tensor_tensor(unit[i][:], picked[i][:], spread_ps[:], ALU.mult)
 
         def first_product(i, k):
             z_ps[i, k] = psum.tile([P, PIECE], F32, name="z_ps", bufs=H_BLOCKS)
@@ -122,11 +125,16 @@ def tile_qdtssolveronnx_kernel(tc, t_store, w_in, b_in, w_out, b_out, offs, out)
                     first_product(i + 1, k)
             scaled = ring.tile([M, PIECE], F32, name="scaled")
             nc.vector.scalar_tensor_tensor(
-                scaled[:], in0=y_ps[:], scalar=b_out_sb[:, 0:1], in1=root[i][:], op0=ALU.add, op1=ALU.mult
+                scaled[:].rearrange("m (b p) -> m b p", b=BLOCKS),
+                in0=y_ps[:].rearrange("m (b p) -> m b p", b=BLOCKS),
+                scalar=b_out_sb[:, 0:1],
+                in1=both[i][:, :, 1, :].rearrange("m p b -> m b p"),
+                op0=ALU.add,
+                op1=ALU.mult,
             )
             clamped = ring.tile([M, PIECE], F32, name="clamped")
             nc.vector.tensor_scalar(clamped[:], scaled[:], -CLAMP, CLAMP, op0=ALU.max, op1=ALU.min)
-            nc.sync.dma_start(out[:, i * PIECE : (i + 1) * PIECE], clamped[:])
+            nc.sync.dma_start(out[:, columns(i)], clamped[:])
 
         for step in range(N_PIECES + NETWORK_LAG):
             if step < N_PIECES:

@@ -31,18 +31,19 @@ def tile_qdtssolveronnx_kernel(tc, t_store, w_in, b_in, w_out, b_out, offs, out)
     ):
         offsets = held.tile([P, N // 16], U16, name="offsets")
         nc.sync.dma_start(offsets[:], offs)
+        store = held.tile([C, S], F32, name="store")
+        nc.sync.dma_start(store[:, : S // 2], t_store[:, : S // 2])
+        nc.scalar.dma_start(store[:, S // 2 :], t_store[:, S // 2 :])
+
+        w_in_sb = held.tile([C, H], BF16, name="w_in_sb")
+        nc.sync.dma_start(w_in_sb[:], w_in)
+        w_out_sb = held.tile([P, H_BLOCKS, M], BF16, name="w_out_sb")
+        nc.scalar.dma_start(w_out_sb[:], w_out.rearrange("(k p) m -> p k m", p=P))
         b_in_sb = held.tile([P, H_BLOCKS], F32, name="b_in_sb")
         b_out_sb = held.tile([M, 1], F32, name="b_out_sb")
         with nc.allow_non_contiguous_dma(reason="a bias has one element to a partition"):
             nc.sync.dma_start(b_in_sb[:], b_in.rearrange("(k p) o -> p (k o)", p=P))
             nc.scalar.dma_start(b_out_sb[:], b_out)
-        w_in_sb = held.tile([C, H], BF16, name="w_in_sb")
-        nc.sync.dma_start(w_in_sb[:], w_in)
-        w_out_sb = held.tile([P, H_BLOCKS, M], BF16, name="w_out_sb")
-        nc.scalar.dma_start(w_out_sb[:], w_out.rearrange("(k p) m -> p k m", p=P))
-        store = held.tile([C, S], F32, name="store")
-        nc.sync.dma_start(store[:, : S // 2], t_store[:, : S // 2])
-        nc.scalar.dma_start(store[:, S // 2 :], t_store[:, S // 2 :])
 
         ones_col = held.tile([C, 1], BF16, name="ones_col")
         nc.vector.memset(ones_col[:], 1.0)

@@ -15,7 +15,6 @@ N_PIECES = N // PIECE
 BLOCKS = PIECE // P
 H_BLOCKS = H // P
 FLOPS = 2 * N * (C * H + H * M)
-PARK = slice(N - 2 * BLOCKS * P, N)
 
 NORMALISE_LAG = 2
 NETWORK_LAG = 5
@@ -31,19 +30,18 @@ def tile_qdtssolveronnx_kernel(tc, t_store, w_in, b_in, w_out, b_out, offs, out)
     ):
         offsets = held.tile([P, N // 16], U16, name="offsets")
         nc.sync.dma_start(offsets[:], offs)
-        store = held.tile([C, S], F32, name="store")
-        nc.sync.dma_start(store[:, : S // 2], t_store[:, : S // 2])
-        nc.scalar.dma_start(store[:, S // 2 :], t_store[:, S // 2 :])
-
-        w_in_sb = held.tile([C, H], BF16, name="w_in_sb")
-        nc.sync.dma_start(w_in_sb[:], w_in)
-        w_out_sb = held.tile([P, H_BLOCKS, M], BF16, name="w_out_sb")
-        nc.scalar.dma_start(w_out_sb[:], w_out.rearrange("(k p) m -> p k m", p=P))
         b_in_sb = held.tile([P, H_BLOCKS], F32, name="b_in_sb")
         b_out_sb = held.tile([M, 1], F32, name="b_out_sb")
         with nc.allow_non_contiguous_dma(reason="a bias has one element to a partition"):
             nc.sync.dma_start(b_in_sb[:], b_in.rearrange("(k p) o -> p (k o)", p=P))
             nc.scalar.dma_start(b_out_sb[:], b_out)
+        w_in_sb = held.tile([C, H], BF16, name="w_in_sb")
+        nc.sync.dma_start(w_in_sb[:], w_in)
+        w_out_sb = held.tile([P, H_BLOCKS, M], BF16, name="w_out_sb")
+        nc.scalar.dma_start(w_out_sb[:], w_out.rearrange("(k p) m -> p k m", p=P))
+        store = held.tile([C, S], F32, name="store")
+        nc.sync.dma_start(store[:, : S // 2], t_store[:, : S // 2])
+        nc.scalar.dma_start(store[:, S // 2 :], t_store[:, S // 2 :])
 
         ones_col = held.tile([C, 1], BF16, name="ones_col")
         nc.vector.memset(ones_col[:], 1.0)
@@ -59,11 +57,8 @@ def tile_qdtssolveronnx_kernel(tc, t_store, w_in, b_in, w_out, b_out, offs, out)
         picked = {}
         powers = {}
         unit = {}
-        both = {}
+        root = {}
         z_ps = {}
-
-        def columns(i):
-            return slice(i * PIECE, (i + 1) * PIECE)
 
         def pick(i):
             picked[i] = per_piece.tile([C, PIECE], F32, name="picked")
@@ -85,24 +80,24 @@ def tile_qdtssolveronnx_kernel(tc, t_store, w_in, b_in, w_out, b_out, offs, out)
                 )
             sums = ring.tile([P, 2, BLOCKS], F32, name="sums")
             nc.vector.tensor_copy(sums[:], sums_ps[:].unsqueeze(1).to_broadcast([P, 2, BLOCKS]))
-            powers[i] = per_piece.tile([P, 2, BLOCKS], F32, name="powers")
+            powers[i] = ring.tile([P, 2, BLOCKS], F32, name="powers", bufs=NORMALISE_LAG + 2)
             nc.gpsimd.tensor_tensor(powers[i][:], sums[:], exponents[:], ALU.pow)
-            nc.sync.dma_start(
-                out[i : i + 1, PARK].rearrange("o (p e) -> (o p) e", e=2 * BLOCKS), powers[i][:]
-            )
 
         def normalise(i):
-            both[i] = per_piece.tile([M, P, 2, BLOCKS], F32, name="both")
-            nc.sync.dma_start(both[i][:], out[i, PARK].partition_broadcast(M))
-            spread_ps = psum.tile([P, PIECE], F32, name="spread_ps", bufs=2)
-            for b in range(BLOCKS):
-                nc.tensor.transpose(
-                    spread_ps[:, b * P : (b + 1) * P],
-                    powers[i][:, 0, b : b + 1].to_broadcast([P, P]),
-                    identity[:],
-                )
+            spread = []
+            for q in range(2):
+                spread_ps = psum.tile([P, PIECE], F32, name="spread_ps", bufs=2)
+                for b in range(BLOCKS):
+                    nc.tensor.transpose(
+                        spread_ps[:, b * P : (b + 1) * P],
+                        powers[i][:, q, b : b + 1].to_broadcast([P, P]),
+                        identity[:],
+                    )
+                spread.append(spread_ps)
             unit[i] = per_piece.tile([C, PIECE], BF16, name="unit")
-            nc.vector.tensor_tensor(unit[i][:], picked[i][:], spread_ps[:], ALU.mult)
+            nc.vector.tensor_tensor(unit[i][:], picked[i][:], spread[0][:], ALU.mult)
+            root[i] = per_piece.tile([M, PIECE], F32, name="root")
+            nc.vector.tensor_copy(root[i][:], spread[1][:])
 
         def first_product(i, k):
             z_ps[i, k] = psum.tile([P, PIECE], F32, name="z_ps", bufs=H_BLOCKS)
@@ -126,16 +121,11 @@ def tile_qdtssolveronnx_kernel(tc, t_store, w_in, b_in, w_out, b_out, offs, out)
                     first_product(i + 1, k)
             scaled = ring.tile([M, PIECE], F32, name="scaled")
             nc.vector.scalar_tensor_tensor(
-                scaled[:].rearrange("m (b p) -> m b p", b=BLOCKS),
-                in0=y_ps[:].rearrange("m (b p) -> m b p", b=BLOCKS),
-                scalar=b_out_sb[:, 0:1],
-                in1=both[i][:, :, 1, :].rearrange("m p b -> m b p"),
-                op0=ALU.add,
-                op1=ALU.mult,
+                scaled[:], in0=y_ps[:], scalar=b_out_sb[:, 0:1], in1=root[i][:], op0=ALU.add, op1=ALU.mult
             )
             clamped = ring.tile([M, PIECE], F32, name="clamped")
             nc.vector.tensor_scalar(clamped[:], scaled[:], -CLAMP, CLAMP, op0=ALU.max, op1=ALU.min)
-            nc.sync.dma_start(out[:, columns(i)], clamped[:])
+            nc.sync.dma_start(out[:, i * PIECE : (i + 1) * PIECE], clamped[:])
 
         for step in range(N_PIECES + NETWORK_LAG):
             if step < N_PIECES:

@@ -14,6 +14,9 @@ PIECE = 512
 N_PIECES = N // PIECE
 BLOCKS = PIECE // P
 H_BLOCKS = H // P
+N_PRODUCTS = N_PIECES * H_BLOCKS
+Z_BANKS = 3
+Y_BANKS = 2
 FLOPS = 2 * N * (C * H + H * M)
 
 NORMALISE_LAG = 2
@@ -99,17 +102,21 @@ def tile_qdtssolveronnx_kernel(tc, t_store, w_in, b_in, w_out, b_out, offs, out)
             root[i] = per_piece.tile([M, PIECE], F32, name="root")
             nc.vector.tensor_copy(root[i][:], spread[1][:])
 
-        def first_product(i, k):
-            z_ps[i, k] = psum.tile([P, PIECE], F32, name="z_ps", bufs=H_BLOCKS)
+        def first_product(n):
+            i, k = divmod(n, H_BLOCKS)
+            z_ps[n] = psum.tile([P, PIECE], F32, name="z_ps", bufs=Z_BANKS)
             nc.tensor.matmul(
-                z_ps[i, k][:], lhsT=w_in_sb[:, k * P : (k + 1) * P], rhs=unit[i][:], start=True, stop=True
+                z_ps[n][:], lhsT=w_in_sb[:, k * P : (k + 1) * P], rhs=unit[i][:], start=True, stop=True
             )
 
         def network(i):
-            y_ps = psum.tile([M, PIECE], F32, name="y_ps")
+            y_ps = psum.tile([M, PIECE], F32, name="y_ps", bufs=Y_BANKS)
             for k in range(H_BLOCKS):
+                n = i * H_BLOCKS + k
                 hidden = per_piece.tile([P, PIECE], BF16, name="hidden")
-                nc.scalar.activation(hidden[:], z_ps[i, k][:], ACT.Silu, bias=b_in_sb[:, k : k + 1])
+                nc.scalar.activation(hidden[:], z_ps[n][:], ACT.Silu, bias=b_in_sb[:, k : k + 1])
+                if n + Z_BANKS < N_PRODUCTS:
+                    first_product(n + Z_BANKS)
                 nc.tensor.matmul(
                     y_ps[:],
                     lhsT=w_out_sb[:, k, :],
@@ -117,8 +124,6 @@ def tile_qdtssolveronnx_kernel(tc, t_store, w_in, b_in, w_out, b_out, offs, out)
                     start=(k == 0),
                     stop=(k == H_BLOCKS - 1),
                 )
-                if i + 1 < N_PIECES:
-                    first_product(i + 1, k)
             scaled = ring.tile([M, PIECE], F32, name="scaled")
             nc.vector.scalar_tensor_tensor(
                 scaled[:], in0=y_ps[:], scalar=b_out_sb[:, 0:1], in1=root[i][:], op0=ALU.add, op1=ALU.mult
@@ -133,7 +138,7 @@ def tile_qdtssolveronnx_kernel(tc, t_store, w_in, b_in, w_out, b_out, offs, out)
             if 0 <= step - NORMALISE_LAG < N_PIECES:
                 normalise(step - NORMALISE_LAG)
             if step == NORMALISE_LAG:
-                for k in range(H_BLOCKS):
-                    first_product(0, k)
+                for n in range(Z_BANKS):
+                    first_product(n)
             if step >= NETWORK_LAG:
                 network(step - NETWORK_LAG)

@@ -38,13 +38,13 @@ def tile_qdtssolveronnx_kernel(tc, t_store, w_in, b_in, w_out, b_out, offs, out)
         with nc.allow_non_contiguous_dma(reason="a bias has one element to a partition"):
             nc.sync.dma_start(b_in_sb[:], b_in.rearrange("(k p) o -> p (k o)", p=P))
             nc.scalar.dma_start(b_out_sb[:], b_out)
+        store = held.tile([C, S], F32, name="store")
+        nc.sync.dma_start(store[:, : S // 2], t_store[:, : S // 2])
+        nc.scalar.dma_start(store[:, S // 2 :], t_store[:, S // 2 :])
         w_in_sb = held.tile([C, H], BF16, name="w_in_sb")
         nc.sync.dma_start(w_in_sb[:], w_in)
         w_out_sb = held.tile([P, H_BLOCKS, M], BF16, name="w_out_sb")
         nc.scalar.dma_start(w_out_sb[:], w_out.rearrange("(k p) m -> p k m", p=P))
-        store = held.tile([C, S], F32, name="store")
-        nc.sync.dma_start(store[:, : S // 2], t_store[:, : S // 2])
-        nc.scalar.dma_start(store[:, S // 2 :], t_store[:, S // 2 :])
 
         ones_col = held.tile([C, 1], BF16, name="ones_col")
         nc.vector.memset(ones_col[:], 1.0)
@@ -110,27 +110,41 @@ def tile_qdtssolveronnx_kernel(tc, t_store, w_in, b_in, w_out, b_out, offs, out)
             )
 
         def network(i):
-            y_ps = psum.tile([M, PIECE], F32, name="y_ps", bufs=Y_BANKS)
+            halves = 2 if i == N_PIECES - 1 else 1
+            width = PIECE // halves
+            columns = [slice(a * width, (a + 1) * width) for a in range(halves)]
+            y_ps = [psum.tile([M, width], F32, name="y_ps", bufs=Y_BANKS) for a in range(halves)]
             for k in range(H_BLOCKS):
                 n = i * H_BLOCKS + k
                 hidden = per_piece.tile([P, PIECE], BF16, name="hidden")
-                nc.scalar.activation(hidden[:], z_ps[n][:], ACT.Silu, bias=b_in_sb[:, k : k + 1])
+                for part in columns if k == H_BLOCKS - 1 else [slice(0, PIECE)]:
+                    nc.scalar.activation(
+                        hidden[:, part], z_ps[n][:, part], ACT.Silu, bias=b_in_sb[:, k : k + 1]
+                    )
                 if n + Z_BANKS < N_PRODUCTS:
                     first_product(n + Z_BANKS)
-                nc.tensor.matmul(
-                    y_ps[:],
-                    lhsT=w_out_sb[:, k, :],
-                    rhs=hidden[:],
-                    start=(k == 0),
-                    stop=(k == H_BLOCKS - 1),
+                for a in range(halves):
+                    nc.tensor.matmul(
+                        y_ps[a][:],
+                        lhsT=w_out_sb[:, k, :],
+                        rhs=hidden[:, columns[a]],
+                        start=(k == 0),
+                        stop=(k == H_BLOCKS - 1),
+                    )
+            for a in range(halves):
+                scaled = ring.tile([M, width], F32, name="scaled")
+                nc.vector.scalar_tensor_tensor(
+                    scaled[:],
+                    in0=y_ps[a][:],
+                    scalar=b_out_sb[:, 0:1],
+                    in1=root[i][:, columns[a]],
+                    op0=ALU.add,
+                    op1=ALU.mult,
                 )
-            scaled = ring.tile([M, PIECE], F32, name="scaled")
-            nc.vector.scalar_tensor_tensor(
-                scaled[:], in0=y_ps[:], scalar=b_out_sb[:, 0:1], in1=root[i][:], op0=ALU.add, op1=ALU.mult
-            )
-            clamped = ring.tile([M, PIECE], F32, name="clamped")
-            nc.vector.tensor_scalar(clamped[:], scaled[:], -CLAMP, CLAMP, op0=ALU.max, op1=ALU.min)
-            nc.sync.dma_start(out[:, i * PIECE : (i + 1) * PIECE], clamped[:])
+                clamped = ring.tile([M, width], F32, name="clamped")
+                nc.vector.tensor_scalar(clamped[:], scaled[:], -CLAMP, CLAMP, op0=ALU.max, op1=ALU.min)
+                first = i * PIECE + a * width
+                nc.sync.dma_start(out[:, first : first + width], clamped[:])
 
         for step in range(N_PIECES + NETWORK_LAG):
             if step < N_PIECES:

@@ -20,7 +20,7 @@ Y_BANKS = 2
 FLOPS = 2 * N * (C * H + H * M)
 
 NORMALISE_LAG = 2
-NETWORK_LAG = 5
+NETWORK_LAG = 4
 
 
 def tile_qdtssolveronnx_kernel(tc, t_store, w_in, b_in, w_out, b_out, offs, out):
@@ -38,13 +38,13 @@ def tile_qdtssolveronnx_kernel(tc, t_store, w_in, b_in, w_out, b_out, offs, out)
         with nc.allow_non_contiguous_dma(reason="a bias has one element to a partition"):
             nc.sync.dma_start(b_in_sb[:], b_in.rearrange("(k p) o -> p (k o)", p=P))
             nc.scalar.dma_start(b_out_sb[:], b_out)
-        store = held.tile([C, S], F32, name="store")
-        nc.sync.dma_start(store[:, : S // 2], t_store[:, : S // 2])
-        nc.scalar.dma_start(store[:, S // 2 :], t_store[:, S // 2 :])
         w_in_sb = held.tile([C, H], BF16, name="w_in_sb")
         nc.sync.dma_start(w_in_sb[:], w_in)
         w_out_sb = held.tile([P, H_BLOCKS, M], BF16, name="w_out_sb")
         nc.scalar.dma_start(w_out_sb[:], w_out.rearrange("(k p) m -> p k m", p=P))
+        store = held.tile([C, S], F32, name="store")
+        nc.sync.dma_start(store[:, : S // 2], t_store[:, : S // 2])
+        nc.scalar.dma_start(store[:, S // 2 :], t_store[:, S // 2 :])
 
         ones_col = held.tile([C, 1], BF16, name="ones_col")
         nc.vector.memset(ones_col[:], 1.0)

@@ -21,6 +21,8 @@ FLOPS = 2 * N * (C * H + H * M)
 
 NORMALISE_LAG = 2
 NETWORK_LAG = 4
+INV_AHEAD = NETWORK_LAG - NORMALISE_LAG
+ROOT_AHEAD = 1
 
 
 def tile_qdtssolveronnx_kernel(tc, t_store, w_in, b_in, w_out, b_out, offs, out):
@@ -83,24 +85,25 @@ def tile_qdtssolveronnx_kernel(tc, t_store, w_in, b_in, w_out, b_out, offs, out)
                 )
             sums = ring.tile([P, 2, BLOCKS], F32, name="sums")
             nc.vector.tensor_copy(sums[:], sums_ps[:].unsqueeze(1).to_broadcast([P, 2, BLOCKS]))
-            powers[i] = ring.tile([P, 2, BLOCKS], F32, name="powers", bufs=NORMALISE_LAG + 2)
+            powers[i] = ring.tile([P, 2, BLOCKS], F32, name="powers", bufs=N_PIECES)
             nc.gpsimd.tensor_tensor(powers[i][:], sums[:], exponents[:], ALU.pow)
 
-        def normalise(i):
-            spread = []
-            for q in range(2):
-                spread_ps = psum.tile([P, PIECE], F32, name="spread_ps", bufs=2)
-                for b in range(BLOCKS):
-                    nc.tensor.transpose(
-                        spread_ps[:, b * P : (b + 1) * P],
-                        powers[i][:, q, b : b + 1].to_broadcast([P, P]),
-                        identity[:],
-                    )
-                spread.append(spread_ps)
-            unit[i] = per_piece.tile([C, PIECE], BF16, name="unit")
-            nc.vector.tensor_tensor(unit[i][:], picked[i][:], spread[0][:], ALU.mult)
-            root[i] = per_piece.tile([M, PIECE], F32, name="root")
-            nc.vector.tensor_copy(root[i][:], spread[1][:])
+        def spread_jobs(i, q):
+            spread_ps = psum.tile([P, PIECE], F32, name="spread_ps", bufs=2)
+            return [(spread_ps, i, q, b) for b in range(BLOCKS)]
+
+        def spread_block(spread_ps, i, q, b):
+            nc.tensor.transpose(
+                spread_ps[:, b * P : (b + 1) * P],
+                powers[i][:, q, b : b + 1].to_broadcast([P, P]),
+                identity[:],
+            )
+            if b == BLOCKS - 1 and q == 0:
+                unit[i] = per_piece.tile([C, PIECE], BF16, name="unit")
+                nc.vector.tensor_tensor(unit[i][:], picked[i][:], spread_ps[:], ALU.mult)
+            if b == BLOCKS - 1 and q == 1:
+                root[i] = per_piece.tile([M, PIECE], F32, name="root")
+                nc.vector.tensor_copy(root[i][:], spread_ps[:])
 
         def first_product(n):
             i, k = divmod(n, H_BLOCKS)
@@ -114,6 +117,11 @@ def tile_qdtssolveronnx_kernel(tc, t_store, w_in, b_in, w_out, b_out, offs, out)
             width = PIECE // halves
             columns = [slice(a * width, (a + 1) * width) for a in range(halves)]
             y_ps = [psum.tile([M, width], F32, name="y_ps", bufs=Y_BANKS) for a in range(halves)]
+            woven = []
+            if i + INV_AHEAD < N_PIECES:
+                woven.extend(spread_jobs(i + INV_AHEAD, 0))
+            if i + ROOT_AHEAD < N_PIECES:
+                woven.extend(spread_jobs(i + ROOT_AHEAD, 1))
             for k in range(H_BLOCKS):
                 n = i * H_BLOCKS + k
                 hidden = per_piece.tile([P, PIECE], BF16, name="hidden")
@@ -123,6 +131,8 @@ def tile_qdtssolveronnx_kernel(tc, t_store, w_in, b_in, w_out, b_out, offs, out)
                     )
                 if n + Z_BANKS < N_PRODUCTS:
                     first_product(n + Z_BANKS)
+                for job in woven[2 * k : 2 * k + 1]:
+                    spread_block(*job)
                 for a in range(halves):
                     nc.tensor.matmul(
                         y_ps[a][:],
@@ -131,6 +141,8 @@ def tile_qdtssolveronnx_kernel(tc, t_store, w_in, b_in, w_out, b_out, offs, out)
                         start=(k == 0),
                         stop=(k == H_BLOCKS - 1),
                     )
+                for job in woven[2 * k + 1 : 2 * k + 2]:
+                    spread_block(*job)
             for a in range(halves):
                 scaled = ring.tile([M, width], F32, name="scaled")
                 nc.vector.scalar_tensor_tensor(
@@ -149,10 +161,15 @@ def tile_qdtssolveronnx_kernel(tc, t_store, w_in, b_in, w_out, b_out, offs, out)
         for step in range(N_PIECES + NETWORK_LAG):
             if step < N_PIECES:
                 pick(step)
-            if 0 <= step - NORMALISE_LAG < N_PIECES:
-                normalise(step - NORMALISE_LAG)
+            if NORMALISE_LAG <= step < NETWORK_LAG:
+                for job in spread_jobs(step - NORMALISE_LAG, 0):
+                    spread_block(*job)
             if step == NORMALISE_LAG:
                 for n in range(Z_BANKS):
                     first_product(n)
+            if step == NETWORK_LAG - 1:
+                for i in range(ROOT_AHEAD):
+                    for job in spread_jobs(i, 1):
+                        spread_block(*job)
             if step >= NETWORK_LAG:
                 network(step - NETWORK_LAG)

@@ -35,18 +35,18 @@ def tile_qdtssolveronnx_kernel(tc, t_store, w_in, b_in, w_out, b_out, offs, out)
     ):
         offsets = held.tile([P, N // 16], U16, name="offsets")
         nc.sync.dma_start(offsets[:], offs)
+        store = held.tile([C, S], F32, name="store")
+        nc.sync.dma_start(store[:, : S // 2], t_store[:, : S // 2])
+        nc.sync.dma_start(store[:, S // 2 :], t_store[:, S // 2 :])
         b_in_sb = held.tile([P, H_BLOCKS], F32, name="b_in_sb")
         b_out_sb = held.tile([M, 1], F32, name="b_out_sb")
         with nc.allow_non_contiguous_dma(reason="a bias has one element to a partition"):
             nc.sync.dma_start(b_in_sb[:], b_in.rearrange("(k p) o -> p (k o)", p=P))
-            nc.scalar.dma_start(b_out_sb[:], b_out)
+            nc.sync.dma_start(b_out_sb[:], b_out)
         w_in_sb = held.tile([C, H], BF16, name="w_in_sb")
         nc.sync.dma_start(w_in_sb[:], w_in)
         w_out_sb = held.tile([P, H_BLOCKS, M], BF16, name="w_out_sb")
-        nc.scalar.dma_start(w_out_sb[:], w_out.rearrange("(k p) m -> p k m", p=P))
-        store = held.tile([C, S], F32, name="store")
-        nc.sync.dma_start(store[:, : S // 2], t_store[:, : S // 2])
-        nc.scalar.dma_start(store[:, S // 2 :], t_store[:, S // 2 :])
+        nc.sync.dma_start(w_out_sb[:], w_out.rearrange("(k p) m -> p k m", p=P))
 
         ones_col = held.tile([C, 1], BF16, name="ones_col")
         nc.vector.memset(ones_col[:], 1.0)

@@ -83,10 +83,11 @@ def tile_qdtssolveronnx_kernel(tc, t_store, w_in, b_in, w_out, b_out, offs, out)
                     start=True,
                     stop=True,
                 )
-            sums = ring.tile([P, 2, BLOCKS], F32, name="sums")
-            nc.vector.tensor_copy(sums[:], sums_ps[:].unsqueeze(1).to_broadcast([P, 2, BLOCKS]))
+            sums = ring.tile([P, BLOCKS], F32, name="sums")
+            nc.vector.tensor_copy(sums[:], sums_ps[:])
             powers[i] = ring.tile([P, 2, BLOCKS], F32, name="powers", bufs=N_PIECES)
-            nc.gpsimd.tensor_tensor(powers[i][:], sums[:], exponents[:], ALU.pow)
+            for q in range(2):
+                nc.gpsimd.tensor_tensor(powers[i][:, q, :], sums[:], exponents[:, q, :], ALU.pow)
 
         def spread_jobs(i, q):
             spread_ps = psum.tile([P, PIECE], F32, name="spread_ps", bufs=2)

@@ -12,9 +12,16 @@ C, S, N, H, M = 128, 4096, 4096, 512, 128
 CLAMP = 2.0
 PIECE = 512
 N_PIECES = N // PIECE
+LOOK_UPS = {0: 1, 1: 1, 2: 2, 4: 2, 6: 2}
 BLOCKS = PIECE // P
 H_BLOCKS = H // P
-N_PRODUCTS = N_PIECES * H_BLOCKS
+PARTS = [(i, 0, PIECE) for i in range(N_PIECES - 1)] + [
+    (N_PIECES - 1, 0, PIECE - P),
+    (N_PIECES - 1, PIECE - P, P),
+]
+FILLS = [(u, [k]) for u in range(len(PARTS) - 1) for k in range(H_BLOCKS)] + [
+    (len(PARTS) - 1, list(range(H_BLOCKS)))
+]
 Z_BANKS = 3
 Y_BANKS = 2
 FLOPS = 2 * N * (C * H + H * M)
@@ -64,16 +71,24 @@ def tile_qdtssolveronnx_kernel(tc, t_store, w_in, b_in, w_out, b_out, offs, out)
         unit = {}
         root = {}
         z_ps = {}
+        fills = list(FILLS)
 
-        def pick(i):
-            picked[i] = per_piece.tile([C, PIECE], F32, name="picked")
+        def look_up(i):
+            if i not in LOOK_UPS:
+                return
+            pieces = LOOK_UPS[i]
+            columns = pieces * PIECE
+            first = i * PIECE
+            many = held.tile([C, columns], F32, name=f"picked_{i}")
             nc.scalar.activation(
-                picked[i][:],
-                store[:].indirect(offsets[:, i * (PIECE // 16) : (i + 1) * (PIECE // 16)]),
-                ACT.Copy,
+                many[:], store[:].indirect(offsets[:, first // 16 : (first + columns) // 16]), ACT.Copy
             )
+            for j in range(pieces):
+                picked[i + j] = many[:, j * PIECE : (j + 1) * PIECE]
+
+        def measure(i):
             squares = ring.tile([C, PIECE], BF16, name="squares")
-            nc.vector.tensor_tensor(squares[:], picked[i][:], picked[i][:], ALU.mult)
+            nc.vector.tensor_tensor(squares[:], picked[i], picked[i], ALU.mult)
             sums_ps = psum.tile([P, BLOCKS], F32, name="sums_ps")
             for b in range(BLOCKS):
                 nc.tensor.matmul(
@@ -101,76 +116,77 @@ def tile_qdtssolveronnx_kernel(tc, t_store, w_in, b_in, w_out, b_out, offs, out)
             )
             if b == BLOCKS - 1 and q == 0:
                 unit[i] = per_piece.tile([C, PIECE], BF16, name="unit")
-                nc.vector.tensor_tensor(unit[i][:], picked[i][:], spread_ps[:], ALU.mult)
+                nc.vector.tensor_tensor(unit[i][:], picked[i], spread_ps[:], ALU.mult)
             if b == BLOCKS - 1 and q == 1:
                 root[i] = per_piece.tile([M, PIECE], F32, name="root")
                 nc.vector.tensor_copy(root[i][:], spread_ps[:])
 
-        def first_product(n):
-            i, k = divmod(n, H_BLOCKS)
-            z_ps[n] = psum.tile([P, PIECE], F32, name="z_ps", bufs=Z_BANKS)
-            nc.tensor.matmul(
-                z_ps[n][:], lhsT=w_in_sb[:, k * P : (k + 1) * P], rhs=unit[i][:], start=True, stop=True
-            )
+        def fill_bank():
+            for u, blocks in fills[:1]:
+                i, first, width = PARTS[u]
+                bank = psum.tile([P, len(blocks), width], F32, name="z_ps", bufs=Z_BANKS)
+                for place, k in enumerate(blocks):
+                    nc.tensor.matmul(
+                        bank[:, place, :],
+                        lhsT=w_in_sb[:, k * P : (k + 1) * P],
+                        rhs=unit[i][:, first : first + width],
+                        start=True,
+                        stop=True,
+                    )
+                    z_ps[u, k] = bank[:, place, :]
+            fills[:1] = []
 
-        def network(i):
-            halves = 2 if i == N_PIECES - 1 else 1
-            width = PIECE // halves
-            columns = [slice(a * width, (a + 1) * width) for a in range(halves)]
-            y_ps = [psum.tile([M, width], F32, name="y_ps", bufs=Y_BANKS) for a in range(halves)]
+        def network(u):
+            i, first, width = PARTS[u]
+            y_ps = psum.tile([M, width], F32, name="y_ps", bufs=Y_BANKS)
             woven = []
             if i + INV_AHEAD < N_PIECES:
                 woven.extend(spread_jobs(i + INV_AHEAD, 0))
             if i + ROOT_AHEAD < N_PIECES:
                 woven.extend(spread_jobs(i + ROOT_AHEAD, 1))
             for k in range(H_BLOCKS):
-                n = i * H_BLOCKS + k
-                hidden = per_piece.tile([P, PIECE], BF16, name="hidden")
-                for part in columns if k == H_BLOCKS - 1 else [slice(0, PIECE)]:
-                    nc.scalar.activation(
-                        hidden[:, part], z_ps[n][:, part], ACT.Silu, bias=b_in_sb[:, k : k + 1]
-                    )
-                if n + Z_BANKS < N_PRODUCTS:
-                    first_product(n + Z_BANKS)
+                hidden = per_piece.tile([P, width], BF16, name="hidden")
+                nc.scalar.activation(hidden[:], z_ps[u, k], ACT.Silu, bias=b_in_sb[:, k : k + 1])
+                fill_bank()
                 for job in woven[2 * k : 2 * k + 1]:
                     spread_block(*job)
-                for a in range(halves):
-                    nc.tensor.matmul(
-                        y_ps[a][:],
-                        lhsT=w_out_sb[:, k, :],
-                        rhs=hidden[:, columns[a]],
-                        start=(k == 0),
-                        stop=(k == H_BLOCKS - 1),
-                    )
+                nc.tensor.matmul(
+                    y_ps[:],
+                    lhsT=w_out_sb[:, k, :],
+                    rhs=hidden[:],
+                    start=(k == 0),
+                    stop=(k == H_BLOCKS - 1),
+                )
                 for job in woven[2 * k + 1 : 2 * k + 2]:
                     spread_block(*job)
-            for a in range(halves):
-                scaled = ring.tile([M, width], F32, name="scaled")
-                nc.vector.scalar_tensor_tensor(
-                    scaled[:],
-                    in0=y_ps[a][:],
-                    scalar=b_out_sb[:, 0:1],
-                    in1=root[i][:, columns[a]],
-                    op0=ALU.add,
-                    op1=ALU.mult,
-                )
-                clamped = ring.tile([M, width], F32, name="clamped")
-                nc.vector.tensor_scalar(clamped[:], scaled[:], -CLAMP, CLAMP, op0=ALU.max, op1=ALU.min)
-                first = i * PIECE + a * width
-                nc.sync.dma_start(out[:, first : first + width], clamped[:])
+            scaled = ring.tile([M, width], F32, name="scaled")
+            nc.vector.scalar_tensor_tensor(
+                scaled[:],
+                in0=y_ps[:],
+                scalar=b_out_sb[:, 0:1],
+                in1=root[i][:, first : first + width],
+                op0=ALU.add,
+                op1=ALU.mult,
+            )
+            clamped = ring.tile([M, width], F32, name="clamped")
+            nc.vector.tensor_scalar(clamped[:], scaled[:], -CLAMP, CLAMP, op0=ALU.max, op1=ALU.min)
+            column = i * PIECE + first
+            nc.sync.dma_start(out[:, column : column + width], clamped[:])
 
-        for step in range(N_PIECES + NETWORK_LAG):
+        for step in range(len(PARTS) + NETWORK_LAG):
             if step < N_PIECES:
-                pick(step)
-            if NORMALISE_LAG <= step < NETWORK_LAG:
-                for job in spread_jobs(step - NORMALISE_LAG, 0):
-                    spread_block(*job)
+                look_up(step)
+                measure(step)
             if step == NORMALISE_LAG:
-                for n in range(Z_BANKS):
-                    first_product(n)
-            if step == NETWORK_LAG - 1:
+                for job in spread_jobs(0, 0):
+                    spread_block(*job)
                 for i in range(ROOT_AHEAD):
                     for job in spread_jobs(i, 1):
                         spread_block(*job)
+                for b in range(Z_BANKS):
+                    fill_bank()
+            if NORMALISE_LAG < step < NETWORK_LAG:
+                for job in spread_jobs(step - NORMALISE_LAG, 0):
+                    spread_block(*job)
             if step >= NETWORK_LAG:
                 network(step - NETWORK_LAG)

@@ -12,7 +12,6 @@ C, S, N, H, M = 128, 4096, 4096, 512, 128
 CLAMP = 2.0
 PIECE = 512
 N_PIECES = N // PIECE
-LOOK_UPS = {0: 1, 1: 1, 2: 2, 4: 2, 6: 2}
 BLOCKS = PIECE // P
 H_BLOCKS = H // P
 PARTS = [(i, 0, PIECE) for i in range(N_PIECES - 1)] + [
@@ -23,6 +22,7 @@ FILLS = [(u, [k]) for u in range(len(PARTS) - 1) for k in range(H_BLOCKS)] + [
     (len(PARTS) - 1, list(range(H_BLOCKS)))
 ]
 Z_BANKS = 3
+PICKED_PIECES = 6
 Y_BANKS = 2
 FLOPS = 2 * N * (C * H + H * M)
 
@@ -74,21 +74,16 @@ def tile_qdtssolveronnx_kernel(tc, t_store, w_in, b_in, w_out, b_out, offs, out)
         fills = list(FILLS)
 
         def look_up(i):
-            if i not in LOOK_UPS:
-                return
-            pieces = LOOK_UPS[i]
-            columns = pieces * PIECE
-            first = i * PIECE
-            many = held.tile([C, columns], F32, name=f"picked_{i}")
+            picked[i] = per_piece.tile([C, PIECE], F32, name="picked", bufs=PICKED_PIECES)
             nc.scalar.activation(
-                many[:], store[:].indirect(offsets[:, first // 16 : (first + columns) // 16]), ACT.Copy
+                picked[i][:],
+                store[:].indirect(offsets[:, i * (PIECE // 16) : (i + 1) * (PIECE // 16)]),
+                ACT.Copy,
             )
-            for j in range(pieces):
-                picked[i + j] = many[:, j * PIECE : (j + 1) * PIECE]
 
         def measure(i):
             squares = ring.tile([C, PIECE], BF16, name="squares")
-            nc.vector.tensor_tensor(squares[:], picked[i], picked[i], ALU.mult)
+            nc.vector.tensor_tensor(squares[:], picked[i][:], picked[i][:], ALU.mult)
             sums_ps = psum.tile([P, BLOCKS], F32, name="sums_ps")
             for b in range(BLOCKS):
                 nc.tensor.matmul(
@@ -104,20 +99,28 @@ def tile_qdtssolveronnx_kernel(tc, t_store, w_in, b_in, w_out, b_out, offs, out)
             for q in range(2):
                 nc.gpsimd.tensor_tensor(powers[i][:, q, :], sums[:], exponents[:, q, :], ALU.pow)
 
-        def spread_jobs(i, q):
-            spread_ps = psum.tile([P, PIECE], F32, name="spread_ps", bufs=2)
-            return [(spread_ps, i, q, b) for b in range(BLOCKS)]
+        def spread_jobs(i, q, tiles=1):
+            jobs = []
+            for a in range(0, BLOCKS, BLOCKS // tiles):
+                z = a + BLOCKS // tiles - 1
+                spread_ps = psum.tile([P, PIECE // tiles], F32, name="spread_ps", bufs=2)
+                jobs.extend([(spread_ps, i, q, a, z, b) for b in range(a, z + 1)])
+            return jobs
 
-        def spread_block(spread_ps, i, q, b):
+        def spread_block(spread_ps, i, q, a, z, b):
             nc.tensor.transpose(
-                spread_ps[:, b * P : (b + 1) * P],
+                spread_ps[:, (b - a) * P : (b - a + 1) * P],
                 powers[i][:, q, b : b + 1].to_broadcast([P, P]),
                 identity[:],
             )
-            if b == BLOCKS - 1 and q == 0:
-                unit[i] = per_piece.tile([C, PIECE], BF16, name="unit")
-                nc.vector.tensor_tensor(unit[i][:], picked[i], spread_ps[:], ALU.mult)
-            if b == BLOCKS - 1 and q == 1:
+            columns = slice(a * P, (z + 1) * P)
+            if b == z and q == 0:
+                if a == 0:
+                    unit[i] = per_piece.tile([C, PIECE], BF16, name="unit")
+                nc.vector.tensor_tensor(
+                    unit[i][:, columns], picked[i][:, columns], spread_ps[:], ALU.mult
+                )
+            if b == z and q == 1:
                 root[i] = per_piece.tile([M, PIECE], F32, name="root")
                 nc.vector.tensor_copy(root[i][:], spread_ps[:])
 
@@ -178,13 +181,13 @@ def tile_qdtssolveronnx_kernel(tc, t_store, w_in, b_in, w_out, b_out, offs, out)
                 look_up(step)
                 measure(step)
             if step == NORMALISE_LAG:
-                for job in spread_jobs(0, 0):
+                for job in spread_jobs(0, 0, tiles=2):
                     spread_block(*job)
+                for b in range(Z_BANKS):
+                    fill_bank()
                 for i in range(ROOT_AHEAD):
                     for job in spread_jobs(i, 1):
                         spread_block(*job)
-                for b in range(Z_BANKS):
-                    fill_bank()
             if NORMALISE_LAG < step < NETWORK_LAG:
                 for job in spread_jobs(step - NORMALISE_LAG, 0):
                     spread_block(*job)

@@ -22,7 +22,7 @@ FILLS = [(u, [k]) for u in range(len(PARTS) - 1) for k in range(H_BLOCKS)] + [
     (len(PARTS) - 1, list(range(H_BLOCKS)))
 ]
 Z_BANKS = 3
-PICKED_PIECES = 6
+LOOK_UPS = {0: 1, 1: 1, 2: 2, 4: 2, 6: 1, 7: 1}
 Y_BANKS = 2
 FLOPS = 2 * N * (C * H + H * M)
 
@@ -74,16 +74,21 @@ def tile_qdtssolveronnx_kernel(tc, t_store, w_in, b_in, w_out, b_out, offs, out)
         fills = list(FILLS)
 
         def look_up(i):
-            picked[i] = per_piece.tile([C, PIECE], F32, name="picked", bufs=PICKED_PIECES)
+            if i not in LOOK_UPS:
+                return
+            pieces = LOOK_UPS[i]
+            wanted = ring.tile([C, pieces * PIECE], F32, name=f"picked_{pieces}", bufs=2)
+            for a in range(pieces):
+                picked[i + a] = wanted[:, a * PIECE : (a + 1) * PIECE]
+            first = i * PIECE
+            last = first + pieces * PIECE
             nc.scalar.activation(
-                picked[i][:],
-                store[:].indirect(offsets[:, i * (PIECE // 16) : (i + 1) * (PIECE // 16)]),
-                ACT.Copy,
+                wanted[:], store[:].indirect(offsets[:, first // 16 : last // 16]), ACT.Copy
             )
 
         def measure(i):
             squares = ring.tile([C, PIECE], BF16, name="squares")
-            nc.vector.tensor_tensor(squares[:], picked[i][:], picked[i][:], ALU.mult)
+            nc.vector.tensor_tensor(squares[:], picked[i], picked[i], ALU.mult)
             sums_ps = psum.tile([P, BLOCKS], F32, name="sums_ps")
             for b in range(BLOCKS):
                 nc.tensor.matmul(

@@ -156,8 +156,6 @@ def tile_qdtssolveronnx_kernel(tc, t_store, w_in, b_in, w_out, b_out, offs, out)
                 hidden = per_piece.tile([P, width], BF16, name="hidden")
                 nc.scalar.activation(hidden[:], z_ps[u, k], ACT.Silu, bias=b_in_sb[:, k : k + 1])
                 fill_bank()
-                for job in woven[2 * k : 2 * k + 1]:
-                    spread_block(*job)
                 nc.tensor.matmul(
                     y_ps[:],
                     lhsT=w_out_sb[:, k, :],
@@ -165,7 +163,7 @@ def tile_qdtssolveronnx_kernel(tc, t_store, w_in, b_in, w_out, b_out, offs, out)
                     start=(k == 0),
                     stop=(k == H_BLOCKS - 1),
                 )
-                for job in woven[2 * k + 1 : 2 * k + 2]:
+                for job in woven[2 * k : 2 * k + 2]:
                     spread_block(*job)
             scaled = ring.tile([M, width], F32, name="scaled")
             nc.vector.scalar_tensor_tensor(

@@ -165,17 +165,24 @@ def tile_qdtssolveronnx_kernel(tc, t_store, w_in, b_in, w_out, b_out, offs, out)
                 )
                 for job in woven[2 * k : 2 * k + 2]:
                     spread_block(*job)
-            scaled = ring.tile([M, width], F32, name="scaled")
-            nc.vector.scalar_tensor_tensor(
-                scaled[:],
-                in0=y_ps[:],
-                scalar=b_out_sb[:, 0:1],
-                in1=root[i][:, first : first + width],
-                op0=ALU.add,
-                op1=ALU.mult,
-            )
+            halves = 2 if u == len(PARTS) - 1 else 1
+            half = width // halves
+            columns = [slice(a * half, (a + 1) * half) for a in range(halves)]
+            scaled = [ring.tile([M, half], F32, name=f"scaled_{a}") for a in range(halves)]
             clamped = ring.tile([M, width], F32, name="clamped")
-            nc.vector.tensor_scalar(clamped[:], scaled[:], -CLAMP, CLAMP, op0=ALU.max, op1=ALU.min)
+            for a in range(halves):
+                nc.vector.scalar_tensor_tensor(
+                    scaled[a][:],
+                    in0=y_ps[:, columns[a]],
+                    scalar=b_out_sb[:, 0:1],
+                    in1=root[i][:, first + a * half : first + (a + 1) * half],
+                    op0=ALU.add,
+                    op1=ALU.mult,
+                )
+            for a in range(halves):
+                nc.vector.tensor_scalar(
+                    clamped[:, columns[a]], scaled[a][:], -CLAMP, CLAMP, op0=ALU.max, op1=ALU.min
+                )
             column = i * PIECE + first
             nc.sync.dma_start(out[:, column : column + width], clamped[:])
 

import concourse.mybir as mybir
from concourse.masks import make_identity

F32 = mybir.dt.float32
BF16 = mybir.dt.bfloat16
U16 = mybir.dt.uint16
ACT = mybir.ActivationFunctionType
ALU = mybir.AluOpType

P = 128
C, S, N, H, M = 128, 4096, 4096, 512, 128
CLAMP = 2.0
PIECE = 512
N_PIECES = N // PIECE
BLOCKS = PIECE // P
H_BLOCKS = H // P
PARTS = [(i, 0, PIECE) for i in range(N_PIECES - 1)] + [
    (N_PIECES - 1, 0, PIECE - P),
    (N_PIECES - 1, PIECE - P, P),
]
FILLS = [(u, [k]) for u in range(len(PARTS) - 1) for k in range(H_BLOCKS)] + [
    (len(PARTS) - 1, list(range(H_BLOCKS)))
]
Z_BANKS = 3
LOOK_UPS = {0: 1, 1: 1, 2: 2, 4: 2, 6: 1, 7: 1}
Y_BANKS = 2
FLOPS = 2 * N * (C * H + H * M)

NORMALISE_LAG = 2
NETWORK_LAG = 4
INV_AHEAD = NETWORK_LAG - NORMALISE_LAG
ROOT_AHEAD = 1


def tile_qdtssolveronnx_kernel(tc, t_store, w_in, b_in, w_out, b_out, offs, out):
    nc = tc.nc
    with (
        tc.tile_pool(name="held", bufs=1) as held,
        tc.tile_pool(name="per_piece", bufs=N_PIECES) as per_piece,
        tc.tile_pool(name="ring", bufs=3) as ring,
        tc.psum_pool(name="psum", bufs=1) as psum,
    ):
        offsets = held.tile([P, N // 16], U16, name="offsets")
        nc.sync.dma_start(offsets[:], offs)
        store = held.tile([C, S], F32, name="store")
        nc.sync.dma_start(store[:, : S // 2], t_store[:, : S // 2])
        nc.sync.dma_start(store[:, S // 2 :], t_store[:, S // 2 :])
        b_in_sb = held.tile([P, H_BLOCKS], F32, name="b_in_sb")
        b_out_sb = held.tile([M, 1], F32, name="b_out_sb")
        with nc.allow_non_contiguous_dma(reason="a bias has one element to a partition"):
            nc.sync.dma_start(b_in_sb[:], b_in.rearrange("(k p) o -> p (k o)", p=P))
            nc.sync.dma_start(b_out_sb[:], b_out)
        w_in_sb = held.tile([C, H], BF16, name="w_in_sb")
        nc.sync.dma_start(w_in_sb[:], w_in)
        w_out_sb = held.tile([P, H_BLOCKS, M], BF16, name="w_out_sb")
        nc.sync.dma_start(w_out_sb[:], w_out.rearrange("(k p) m -> p k m", p=P))

        ones_col = held.tile([C, 1], BF16, name="ones_col")
        nc.vector.memset(ones_col[:], 1.0)
        exponents = held.tile([P, 2, BLOCKS], F32, name="exponents")
        nc.vector.memset(exponents[:, 0, :], -0.5)
        nc.vector.memset(exponents[:, 1, :], 0.25)
        identity = held.tile([P, P], F32, name="identity")
        make_identity(nc, identity[:])

        warm = held.tile([P, 1], F32, name="warm")
        nc.scalar.activation(warm[:], exponents[:, 0, 0:1], ACT.Silu)

        picked = {}
        powers = {}
        unit = {}
        root = {}
        z_ps = {}
        fills = list(FILLS)

        def look_up(i):
            if i not in LOOK_UPS:
                return
            pieces = LOOK_UPS[i]
            wanted = ring.tile([C, pieces * PIECE], F32, name=f"picked_{pieces}", bufs=2)
            for a in range(pieces):
                picked[i + a] = wanted[:, a * PIECE : (a + 1) * PIECE]
            first = i * PIECE
            last = first + pieces * PIECE
            nc.scalar.activation(
                wanted[:], store[:].indirect(offsets[:, first // 16 : last // 16]), ACT.Copy
            )

        def measure(i):
            squares = ring.tile([C, PIECE], BF16, name="squares")
            nc.vector.tensor_tensor(squares[:], picked[i], picked[i], ALU.mult)
            sums_ps = psum.tile([P, BLOCKS], F32, name="sums_ps")
            for b in range(BLOCKS):
                nc.tensor.matmul(
                    sums_ps[:, b : b + 1],
                    lhsT=squares[:, b * P : (b + 1) * P],
                    rhs=ones_col[:],
                    start=True,
                    stop=True,
                )
            sums = ring.tile([P, BLOCKS], F32, name="sums")
            nc.vector.tensor_copy(sums[:], sums_ps[:])
            powers[i] = ring.tile([P, 2, BLOCKS], F32, name="powers", bufs=N_PIECES)
            for q in range(2):
                nc.gpsimd.tensor_tensor(powers[i][:, q, :], sums[:], exponents[:, q, :], ALU.pow)

        def spread_jobs(i, q, tiles=1):
            jobs = []
            for a in range(0, BLOCKS, BLOCKS // tiles):
                z = a + BLOCKS // tiles - 1
                spread_ps = psum.tile([P, PIECE // tiles], F32, name="spread_ps", bufs=2)
                jobs.extend([(spread_ps, i, q, a, z, b) for b in range(a, z + 1)])
            return jobs

        def spread_block(spread_ps, i, q, a, z, b):
            nc.tensor.transpose(
                spread_ps[:, (b - a) * P : (b - a + 1) * P],
                powers[i][:, q, b : b + 1].to_broadcast([P, P]),
                identity[:],
            )
            columns = slice(a * P, (z + 1) * P)
            if b == z and q == 0:
                if a == 0:
                    unit[i] = per_piece.tile([C, PIECE], BF16, name="unit")
                nc.vector.tensor_tensor(
                    unit[i][:, columns], picked[i][:, columns], spread_ps[:], ALU.mult
                )
            if b == z and q == 1:
                root[i] = per_piece.tile([M, PIECE], F32, name="root")
                nc.vector.tensor_copy(root[i][:], spread_ps[:])

        def fill_bank():
            for u, blocks in fills[:1]:
                i, first, width = PARTS[u]
                bank = psum.tile([P, len(blocks), width], F32, name="z_ps", bufs=Z_BANKS)
                for place, k in enumerate(blocks):
                    nc.tensor.matmul(
                        bank[:, place, :],
                        lhsT=w_in_sb[:, k * P : (k + 1) * P],
                        rhs=unit[i][:, first : first + width],
                        start=True,
                        stop=True,
                    )
                    z_ps[u, k] = bank[:, place, :]
            fills[:1] = []

        def network(u):
            i, first, width = PARTS[u]
            y_ps = psum.tile([M, width], F32, name="y_ps", bufs=Y_BANKS)
            woven = []
            if i + INV_AHEAD < N_PIECES:
                woven.extend(spread_jobs(i + INV_AHEAD, 0))
            if i + ROOT_AHEAD < N_PIECES:
                woven.extend(spread_jobs(i + ROOT_AHEAD, 1))
            for k in range(H_BLOCKS):
                hidden = per_piece.tile([P, width], BF16, name="hidden")
                nc.scalar.activation(hidden[:], z_ps[u, k], ACT.Silu, bias=b_in_sb[:, k : k + 1])
                fill_bank()
                nc.tensor.matmul(
                    y_ps[:],
                    lhsT=w_out_sb[:, k, :],
                    rhs=hidden[:],
                    start=(k == 0),
                    stop=(k == H_BLOCKS - 1),
                )
                for job in woven[2 * k : 2 * k + 2]:
                    spread_block(*job)
            halves = 2 if u == len(PARTS) - 1 else 1
            half = width // halves
            columns = [slice(a * half, (a + 1) * half) for a in range(halves)]
            scaled = [ring.tile([M, half], F32, name=f"scaled_{a}") for a in range(halves)]
            clamped = ring.tile([M, width], F32, name="clamped")
            for a in range(halves):
                nc.vector.scalar_tensor_tensor(
                    scaled[a][:],
                    in0=y_ps[:, columns[a]],
                    scalar=b_out_sb[:, 0:1],
                    in1=root[i][:, first + a * half : first + (a + 1) * half],
                    op0=ALU.add,
                    op1=ALU.mult,
                )
            for a in range(halves):
                nc.vector.tensor_scalar(
                    clamped[:, columns[a]], scaled[a][:], -CLAMP, CLAMP, op0=ALU.max, op1=ALU.min
                )
            column = i * PIECE + first
            nc.sync.dma_start(out[:, column : column + width], clamped[:])

        for step in range(len(PARTS) + NETWORK_LAG):
            if step < N_PIECES:
                look_up(step)
                measure(step)
            if step == NORMALISE_LAG:
                for job in spread_jobs(0, 0, tiles=2):
                    spread_block(*job)
                for b in range(Z_BANKS):
                    fill_bank()
                for i in range(ROOT_AHEAD):
                    for job in spread_jobs(i, 1):
                        spread_block(*job)
            if NORMALISE_LAG < step < NETWORK_LAG:
                for job in spread_jobs(step - NORMALISE_LAG, 0):
                    spread_block(*job)
            if step >= NETWORK_LAG:
                network(step - NETWORK_LAG)
